import numpy as np
import ml_dtypes


def mxq(x, axis, fmt="e4m3"):
    dtype, down = {"e4m3": (ml_dtypes.float8_e4m3fn, 7), "e5m2": (ml_dtypes.float8_e5m2, 14)}[fmt]
    v = np.moveaxis(np.asarray(x, np.float32).astype(ml_dtypes.bfloat16).astype(np.float64), axis, -1)
    blocks = v.reshape(v.shape[:-1] + (-1, 32))
    amax = np.abs(blocks).max(-1, keepdims=True)
    byte = np.maximum(np.where(amax > 0, np.frexp(amax)[1] - 1 + 127, 0) - down, 1)
    scale = np.exp2(byte - 127.0)
    codes = (blocks / scale).astype(np.float32).astype(dtype).astype(np.float64)
    return np.moveaxis((codes * scale).reshape(v.shape), -1, axis)


WIDE = False


def mx_kscale(k):
    if not WIDE:
        return np.ones(k)
    levels = np.array([10, -10, 5, -5, 0])
    a = np.random.permutation(np.resize(levels, k // 512 * 4)).reshape(k // 512, 4)
    idx = np.arange(k)
    return np.exp2(a[idx // 512, idx % 128 // 32])


BF16 = ml_dtypes.bfloat16


def bf(x):
    return np.asarray(x, np.float32).astype(BF16)


def f64(x):
    return np.asarray(x).astype(np.float64)


B, S, H, NH, NKV, HD = 2, 512, 2048, 16, 4, 128
EPS = 1e-6


def rms_norm(x, w):
    var = np.mean(x * x, axis=-1, keepdims=True)
    return x * (1.0 / np.sqrt(var + EPS)) * w


def rotate_half(x):
    x1, x2 = np.split(x, 2, axis=-1)
    return np.concatenate([-x2, x1], axis=-1)


def setup_inputs():
    s = mx_kscale(H)
    inv_freq = 1.0 / (10000.0 ** (np.arange(0, HD, 2) / HD))
    freqs = np.arange(S)[:, None] * inv_freq[None, :]
    emb = np.concatenate([freqs, freqs], axis=-1)
    return {"hidden_states": bf(np.random.standard_normal((B, S, H)) * s),
            "cos": bf(np.cos(emb)),
            "sin": bf(np.sin(emb)),
            "wq": bf(np.random.standard_normal((NH * HD, H)) / np.sqrt(H) / s[None, :]),
            "wk": bf(np.random.standard_normal((NKV * HD, H)) / np.sqrt(H) / s[None, :]),
            "q_norm_w": bf(1.0 + 0.1 * np.random.standard_normal(HD)),
            "k_norm_w": bf(1.0 + 0.1 * np.random.standard_normal(HD)),
            "ssmax_scale": bf((1.0 + 0.2 * np.random.standard_normal((1, NH, 1, 1))) / np.log(S))}


def reference(hidden_states, cos, sin, wq, wk, q_norm_w, k_norm_w, ssmax_scale):
    xq = mxq(f64(hidden_states), 2, "e4m3")
    q = (xq @ mxq(f64(wq), 1, "e4m3").T).reshape(B, S, NH, HD)
    k = (xq @ mxq(f64(wk), 1, "e4m3").T).reshape(B, S, NKV, HD)
    q = rms_norm(q, f64(q_norm_w)).transpose(0, 2, 1, 3)
    k = rms_norm(k, f64(k_norm_w)).transpose(0, 2, 1, 3)
    c = f64(cos)[None, None]
    sn = f64(sin)[None, None]
    q = q * c + rotate_half(q) * sn
    k = k * c + rotate_half(k) * sn
    q = q * (f64(ssmax_scale) * np.log(S))
    return q, k

@@ -1,0 +1,226 @@
+from contextlib import ExitStack
+import math
+
+import concourse.mybir as mybir
+from concourse.masks import make_identity
+
+F32 = mybir.dt.float32
+BF16 = mybir.dt.bfloat16
+U32 = mybir.dt.uint32
+U8 = mybir.dt.uint8
+FP8X4 = mybir.dt.float8_e4m3fn_x4
+ACT = mybir.ActivationFunctionType
+ALU = mybir.AluOpType
+
+P = 128
+BATCH, SEQ, HIDDEN = 2, 512, 2048
+Q_HEADS, KV_HEADS, HEAD_DIM = 16, 4, 128
+HALF = HEAD_DIM // 2
+EPS = 1e-6
+
+K_PASS = 4 * P
+PASSES = HIDDEN // K_PASS
+WORDS_PER_PASS = K_PASS // 2
+SEQ_TILES = SEQ // P
+TOKEN_TILES = BATCH * SEQ_TILES
+CHUNK_HEADS = 4
+CHUNK = CHUNK_HEADS * HEAD_DIM
+Q_CHUNKS = Q_HEADS // CHUNK_HEADS
+CHUNKS = Q_CHUNKS + KV_HEADS // CHUNK_HEADS
+HEADS = Q_HEADS + KV_HEADS
+ROW_TILES = TOKEN_TILES + CHUNKS * CHUNK_HEADS
+
+FLOPS = 2 * BATCH * SEQ * HIDDEN * HEADS * HEAD_DIM
+
+
+def tile_biboattention_pa_kernel(
+    tc, hidden_states, cos, sin, wq, wk, q_norm_w, k_norm_w, ssmax_scale, out_0, out_1
+):
+    nc = tc.nc
+    with ExitStack() as ctx:
+        const = ctx.enter_context(tc.tile_pool(name="const", bufs=1))
+        raw_pool = ctx.enter_context(tc.tile_pool(name="raw", bufs=ROW_TILES))
+        grouped_pool = ctx.enter_context(tc.tile_pool(name="grouped", bufs=3))
+        w_pool = ctx.enter_context(tc.tile_pool(name="w_mx", bufs=3))
+        small = ctx.enter_context(tc.tile_pool(name="small", bufs=4))
+        prod_pool = ctx.enter_context(tc.tile_pool(name="prod", bufs=3))
+        result_pool = ctx.enter_context(tc.tile_pool(name="result", bufs=3))
+        flip_psum = ctx.enter_context(tc.psum_pool(name="flip_psum", bufs=4))
+        acc_psum = ctx.enter_context(tc.psum_pool(name="acc_psum", bufs=4))
+
+        x_view = hidden_states.rearrange("b (p t) k -> b t p k", t=SEQ_TILES)
+        wq_view = wq.rearrange("(n j p) k -> n j p k", j=CHUNK_HEADS, p=P)
+        wk_view = wk.rearrange("(j p) k -> j p k", p=P)
+
+        x_raw = []
+        w_raw = []
+
+        def load_w(n):
+            for j in range(CHUNK_HEADS):
+                tile_w = raw_pool.tile([P, HIDDEN], BF16, name="raw")
+                nc.sync.dma_start(out=tile_w[:], in_=wq_view[n, j] if n < Q_CHUNKS else wk_view[j])
+                w_raw.append(tile_w)
+
+        load_w(0)
+        for m in range(TOKEN_TILES):
+            tile_x = raw_pool.tile([P, HIDDEN], BF16, name="raw")
+            nc.sync.dma_start(out=tile_x[:], in_=x_view[m // SEQ_TILES, m % SEQ_TILES])
+            x_raw.append(tile_x)
+        for n in range(1, CHUNKS):
+            load_w(n)
+
+        cos_sb = const.tile([P, SEQ_TILES, HEAD_DIM], BF16)
+        sin_sb = const.tile([P, SEQ_TILES, HEAD_DIM], BF16)
+        nc.scalar.dma_start(out=cos_sb[:], in_=cos.rearrange("(p t) d -> p t d", t=SEQ_TILES))
+        nc.scalar.dma_start(out=sin_sb[:], in_=sin.rearrange("(p t) d -> p t d", t=SEQ_TILES))
+        norm_w = const.tile([P, 2, HEAD_DIM], BF16)
+        nc.gpsimd.dma_start(out=norm_w[:, 0, :], in_=q_norm_w.partition_broadcast(P))
+        nc.gpsimd.dma_start(out=norm_w[:, 1, :], in_=k_norm_w.partition_broadcast(P))
+        ssmax_sb = const.tile([P, Q_HEADS], BF16)
+        nc.gpsimd.dma_start(
+            out=ssmax_sb[:], in_=ssmax_scale.rearrange("a h b c -> (a h b c)").partition_broadcast(P)
+        )
+
+        ident = const.tile([P, P], F32)
+        make_identity(nc, ident[:])
+
+        one = const.tile([P, 1], F32)
+        nc.vector.memset(one[:], 1.0)
+        warm = const.tile([P, 1], F32)
+        nc.scalar.activation(out=warm[:], in_=one[:], func=ACT.Abs_reciprocal_sqrt)
+
+        gain = const.tile([P, HEADS], F32)
+        nc.vector.memset(gain[:, Q_HEADS:], 1.0)
+        nc.vector.tensor_scalar_mul(out=gain[:, :Q_HEADS], in0=ssmax_sb[:], scalar1=math.log(SEQ))
+        table = const.tile([P, SEQ_TILES, 2, 2, HEAD_DIM], F32)
+        for kind in range(2):
+            nc.vector.tensor_tensor(
+                out=table[:, :, kind, 0, :],
+                in0=cos_sb[:],
+                in1=norm_w[:, kind, :].unsqueeze(1).to_broadcast([P, SEQ_TILES, HEAD_DIM]),
+                op=ALU.mult,
+            )
+            nc.vector.tensor_tensor(
+                out=table[:, :, kind, 1, :HALF],
+                in0=sin_sb[:, :, HALF:],
+                in1=norm_w[:, kind, :HALF].unsqueeze(1).to_broadcast([P, SEQ_TILES, HALF]),
+                op=ALU.mult,
+            )
+            nc.vector.scalar_tensor_tensor(
+                out=table[:, :, kind, 1, HALF:],
+                in0=sin_sb[:, :, :HALF],
+                scalar=-1.0,
+                in1=norm_w[:, kind, HALF:].unsqueeze(1).to_broadcast([P, SEQ_TILES, HALF]),
+                op0=ALU.mult,
+                op1=ALU.mult,
+            )
+
+        x_codes = const.tile([P, TOKEN_TILES, PASSES, P], U32, align_bytes=64)
+        x_scales = const.tile([P, TOKEN_TILES, PASSES, P], U8, align_bytes=64)
+
+        def quantise_row_tile(raw, codes, scales):
+            words = raw[:].bitcast(F32)
+            grouped = grouped_pool.tile([P, PASSES, P, 2], F32, align_bytes=64)
+            for bank in range(PASSES // 2):
+                flipped = flip_psum.tile([P, 2, 2, P], F32)
+                for a in range(2):
+                    for u in range(2):
+                        first = (2 * bank + a) * WORDS_PER_PASS + u * P
+                        nc.tensor.transpose(flipped[:, a, u, :], words[:, first : first + P], ident[:])
+                nc.scalar.copy(
+                    out=grouped[:, 2 * bank : 2 * bank + 2, :, :],
+                    in_=flipped[:].rearrange("p a u r -> p a r u"),
+                )
+            for g in range(PASSES):
+                nc.vector.quantize_mx(
+                    out=codes[:, g, :].bitcast(FP8X4),
+                    scales=scales[:, g, :],
+                    in_=grouped[:, g, :, :].rearrange("p r u -> p (r u)").bitcast(BF16),
+                )
+
+        w_mx = {}
+
+        def prepare_w(n, j):
+            if j == 0:
+                w_codes = w_pool.tile([P, PASSES, CHUNK], U32, align_bytes=64)
+                w_scales = w_pool.tile([P, PASSES, CHUNK], U8, align_bytes=64)
+                w_mx[n] = (w_codes, w_scales)
+            w_codes, w_scales = w_mx[n]
+            rows = slice(j * P, (j + 1) * P)
+            quantise_row_tile(w_raw[n * CHUNK_HEADS + j], w_codes[:, :, rows], w_scales[:, :, rows])
+
+        def prepare_x(m):
+            quantise_row_tile(x_raw[m], x_codes[:, m], x_scales[:, m])
+
+        results = {}
+
+        def project(m, n):
+            b, t = m // SEQ_TILES, m % SEQ_TILES
+            kind = 0 if n < Q_CHUNKS else 1
+            w_codes, w_scales = w_mx[n]
+            acc = acc_psum.tile([P, CHUNK], F32)
+            for g in range(PASSES):
+                nc.tensor.matmul_mx(
+                    out=acc[:],
+                    lhsT=x_codes[:, m, g, :].bitcast(FP8X4),
+                    lhsT_scale=x_scales[:, m, g, :],
+                    rhs=w_codes[:, g, :].bitcast(FP8X4),
+                    rhs_scale=w_scales[:, g, :],
+                    start=(g == 0),
+                    stop=(g == PASSES - 1),
+                )
+            sumsq = small.tile([P, CHUNK_HEADS], F32)
+            for h in range(CHUNK_HEADS):
+                squares = small.tile([P, HEAD_DIM], F32)
+                nc.scalar.activation(
+                    out=squares[:],
+                    in_=acc[:, h * HEAD_DIM : (h + 1) * HEAD_DIM],
+                    func=ACT.Square,
+                    accum_out=sumsq[:, h : h + 1],
+                )
+            rstd = small.tile([P, CHUNK_HEADS], F32)
+            nc.scalar.activation(
+                out=rstd[:], in_=sumsq[:], func=ACT.Abs_reciprocal_sqrt, scale=1.0 / HEAD_DIM, bias=EPS
+            )
+            factor = small.tile([P, CHUNK_HEADS], F32)
+            nc.vector.tensor_mul(
+                out=factor[:], in0=rstd[:], in1=gain[:, n * CHUNK_HEADS : (n + 1) * CHUNK_HEADS]
+            )
+            prod = prod_pool.tile([P, CHUNK_HEADS, 2, HEAD_DIM], F32)
+            for h in range(CHUNK_HEADS):
+                nc.vector.scalar_tensor_tensor(
+                    out=prod[:, h, :, :],
+                    in0=acc[:, h * HEAD_DIM : (h + 1) * HEAD_DIM].unsqueeze(1).to_broadcast([P, 2, HEAD_DIM]),
+                    scalar=factor[:, h : h + 1],
+                    in1=table[:, t, kind, :, :],
+                    op0=ALU.mult,
+                    op1=ALU.mult,
+                )
+            if t == 0:
+                result = result_pool.tile([P, CHUNK_HEADS, SEQ_TILES, HEAD_DIM], F32)
+                results[0] = result
+            result = results[0]
+            nc.gpsimd.tensor_tensor(
+                out=result[:, :, t, :HALF], in0=prod[:, :, 0, :HALF], in1=prod[:, :, 1, HALF:], op=ALU.add
+            )
+            nc.gpsimd.tensor_tensor(
+                out=result[:, :, t, HALF:], in0=prod[:, :, 0, HALF:], in1=prod[:, :, 1, :HALF], op=ALU.add
+            )
+            if t == SEQ_TILES - 1:
+                if kind == 0:
+                    heads = out_0[b, n * CHUNK_HEADS : (n + 1) * CHUNK_HEADS]
+                else:
+                    heads = out_1[b]
+                nc.sync.dma_start(
+                    out=heads.rearrange("h (p t) d -> p h t d", t=SEQ_TILES), in_=result[:]
+                )
+
+        for j in range(CHUNK_HEADS):
+            prepare_w(0, j)
+        for n in range(CHUNKS):
+            for m in range(TOKEN_TILES):
+                if n == 0:
+                    prepare_x(m)
+                if n + 1 < CHUNKS and m >= TOKEN_TILES - CHUNK_HEADS:
+                    prepare_w(n + 1, m - (TOKEN_TILES - CHUNK_HEADS))
+                project(m, n)

@@ -30,6 +30,9 @@ CHUNKS = Q_CHUNKS + KV_HEADS // CHUNK_HEADS
 HEADS = Q_HEADS + KV_HEADS
 ROW_TILES = TOKEN_TILES + CHUNKS * CHUNK_HEADS
 
+X_LEAD = 2
+GPSIMD_TILES = 3
+
 FLOPS = 2 * BATCH * SEQ * HIDDEN * HEADS * HEAD_DIM
 
 
@@ -47,40 +50,55 @@ def tile_biboattention_pa_kernel(
         result_pool = ctx.enter_context(tc.tile_pool(name="result", bufs=3))
         flip_psum = ctx.enter_context(tc.psum_pool(name="flip_psum", bufs=4))
         acc_psum = ctx.enter_context(tc.psum_pool(name="acc_psum", bufs=4))
+        ctx.enter_context(tc.manual_schedule())
 
         x_view = hidden_states.rearrange("b (p t) k -> b t p k", t=SEQ_TILES)
         wq_view = wq.rearrange("(n j p) k -> n j p k", j=CHUNK_HEADS, p=P)
         wk_view = wk.rearrange("(j p) k -> j p k", p=P)
 
-        x_raw = []
-        w_raw = []
-
-        def load_w(n):
+        def lead_in(on_x, on_w):
             for j in range(CHUNK_HEADS):
-                tile_w = raw_pool.tile([P, HIDDEN], BF16, name="raw")
-                nc.sync.dma_start(out=tile_w[:], in_=wq_view[n, j] if n < Q_CHUNKS else wk_view[j])
-                w_raw.append(tile_w)
+                on_w(0, j)
+            for m in range(X_LEAD):
+                on_x(m)
 
-        load_w(0)
-        for m in range(TOKEN_TILES):
-            tile_x = raw_pool.tile([P, HIDDEN], BF16, name="raw")
-            nc.sync.dma_start(out=tile_x[:], in_=x_view[m // SEQ_TILES, m % SEQ_TILES])
-            x_raw.append(tile_x)
-        for n in range(1, CHUNKS):
-            load_w(n)
+        def all_banks(on_x, on_w, on_bank):
+            for n in range(CHUNKS):
+                for m in range(TOKEN_TILES):
+                    if n == 0 and m + X_LEAD < TOKEN_TILES:
+                        on_x(m + X_LEAD)
+                    if n + 1 < CHUNKS and m < CHUNK_HEADS:
+                        on_w(n + 1, m)
+                    on_bank(m, n)
+
+        x_raw = {}
+        w_raw = {}
+
+        def load_x(m):
+            x_raw[m] = raw_pool.tile([P, HIDDEN], BF16, name="raw")
+            nc.sync.dma_start(out=x_raw[m][:], in_=x_view[m // SEQ_TILES, m % SEQ_TILES])
+
+        def load_w(n, j):
+            w_raw[n, j] = raw_pool.tile([P, HIDDEN], BF16, name="raw")
+            nc.sync.dma_start(out=w_raw[n, j][:], in_=wq_view[n, j] if n < Q_CHUNKS else wk_view[j])
+
+        lead_in(load_x, load_w)
+        all_banks(load_x, load_w, lambda m, n: None)
 
         cos_sb = const.tile([P, SEQ_TILES, HEAD_DIM], BF16)
         sin_sb = const.tile([P, SEQ_TILES, HEAD_DIM], BF16)
         nc.scalar.dma_start(out=cos_sb[:], in_=cos.rearrange("(p t) d -> p t d", t=SEQ_TILES))
         nc.scalar.dma_start(out=sin_sb[:], in_=sin.rearrange("(p t) d -> p t d", t=SEQ_TILES))
-        norm_w = const.tile([P, 2, HEAD_DIM], BF16)
-        nc.gpsimd.dma_start(out=norm_w[:, 0, :], in_=q_norm_w.partition_broadcast(P))
-        nc.gpsimd.dma_start(out=norm_w[:, 1, :], in_=k_norm_w.partition_broadcast(P))
-        ssmax_sb = const.tile([P, Q_HEADS], BF16)
-        nc.gpsimd.dma_start(
-            out=ssmax_sb[:], in_=ssmax_scale.rearrange("a h b c -> (a h b c)").partition_broadcast(P)
+        vectors = const.tile([P, CHUNK], BF16)
+        nc.vector.memset(vectors[:], 0.0)
+        ones = const.tile([P, P], BF16)
+        nc.vector.memset(ones[:], 1.0)
+        nc.scalar.dma_start(out=vectors[0:1, 0:HEAD_DIM], in_=q_norm_w.unsqueeze(0))
+        nc.scalar.dma_start(out=vectors[0:1, HEAD_DIM : 2 * HEAD_DIM], in_=k_norm_w.unsqueeze(0))
+        nc.scalar.dma_start(
+            out=vectors[0:1, 2 * HEAD_DIM : 2 * HEAD_DIM + Q_HEADS],
+            in_=ssmax_scale.rearrange("a h b c -> (a b c) h"),
         )
-
         ident = const.tile([P, P], F32)
         make_identity(nc, ident[:])
 
@@ -90,30 +108,35 @@ def tile_biboattention_pa_kernel(
         nc.scalar.activation(out=warm[:], in_=one[:], func=ACT.Abs_reciprocal_sqrt)
 
         gain = const.tile([P, HEADS], F32)
-        nc.vector.memset(gain[:, Q_HEADS:], 1.0)
-        nc.vector.tensor_scalar_mul(out=gain[:, :Q_HEADS], in0=ssmax_sb[:], scalar1=math.log(SEQ))
         table = const.tile([P, SEQ_TILES, 2, 2, HEAD_DIM], F32)
-        for kind in range(2):
-            nc.vector.tensor_tensor(
-                out=table[:, :, kind, 0, :],
-                in0=cos_sb[:],
-                in1=norm_w[:, kind, :].unsqueeze(1).to_broadcast([P, SEQ_TILES, HEAD_DIM]),
-                op=ALU.mult,
-            )
-            nc.vector.tensor_tensor(
-                out=table[:, :, kind, 1, :HALF],
-                in0=sin_sb[:, :, HALF:],
-                in1=norm_w[:, kind, :HALF].unsqueeze(1).to_broadcast([P, SEQ_TILES, HALF]),
-                op=ALU.mult,
-            )
-            nc.vector.scalar_tensor_tensor(
-                out=table[:, :, kind, 1, HALF:],
-                in0=sin_sb[:, :, :HALF],
-                scalar=-1.0,
-                in1=norm_w[:, kind, HALF:].unsqueeze(1).to_broadcast([P, SEQ_TILES, HALF]),
-                op0=ALU.mult,
-                op1=ALU.mult,
-            )
+
+        def build_tables():
+          spread = flip_psum.tile([P, CHUNK], F32, name="flipped")
+          nc.tensor.matmul(out=spread[:], lhsT=ones[:], rhs=vectors[:], start=True, stop=True)
+          norm_w = spread[:, : 2 * HEAD_DIM].rearrange("p (kind d) -> p kind d", kind=2)
+          nc.vector.memset(gain[:, Q_HEADS:], 1.0)
+          nc.vector.tensor_scalar_mul(out=gain[:, :Q_HEADS], in0=spread[:, 2 * HEAD_DIM : 2 * HEAD_DIM + Q_HEADS], scalar1=math.log(SEQ))
+          for kind in range(2):
+              nc.vector.tensor_tensor(
+                  out=table[:, :, kind, 0, :],
+                  in0=cos_sb[:],
+                  in1=norm_w[:, kind, :].unsqueeze(1).to_broadcast([P, SEQ_TILES, HEAD_DIM]),
+                  op=ALU.mult,
+              )
+              nc.vector.tensor_tensor(
+                  out=table[:, :, kind, 1, :HALF],
+                  in0=sin_sb[:, :, HALF:],
+                  in1=norm_w[:, kind, :HALF].unsqueeze(1).to_broadcast([P, SEQ_TILES, HALF]),
+                  op=ALU.mult,
+              )
+              nc.vector.scalar_tensor_tensor(
+                  out=table[:, :, kind, 1, HALF:],
+                  in0=sin_sb[:, :, :HALF],
+                  scalar=-1.0,
+                  in1=norm_w[:, kind, HALF:].unsqueeze(1).to_broadcast([P, SEQ_TILES, HALF]),
+                  op0=ALU.mult,
+                  op1=ALU.mult,
+              )
 
         x_codes = const.tile([P, TOKEN_TILES, PASSES, P], U32, align_bytes=64)
         x_scales = const.tile([P, TOKEN_TILES, PASSES, P], U8, align_bytes=64)
@@ -147,7 +170,7 @@ def tile_biboattention_pa_kernel(
                 w_mx[n] = (w_codes, w_scales)
             w_codes, w_scales = w_mx[n]
             rows = slice(j * P, (j + 1) * P)
-            quantise_row_tile(w_raw[n * CHUNK_HEADS + j], w_codes[:, :, rows], w_scales[:, :, rows])
+            quantise_row_tile(w_raw[n, j], w_codes[:, :, rows], w_scales[:, :, rows])
 
         def prepare_x(m):
             quantise_row_tile(x_raw[m], x_codes[:, m], x_scales[:, m])
@@ -200,27 +223,23 @@ def tile_biboattention_pa_kernel(
                 result = result_pool.tile([P, CHUNK_HEADS, SEQ_TILES, HEAD_DIM], F32)
                 results[0] = result
             result = results[0]
-            nc.gpsimd.tensor_tensor(
+            adder = nc.gpsimd if t < GPSIMD_TILES else nc.vector
+            adder.tensor_tensor(
                 out=result[:, :, t, :HALF], in0=prod[:, :, 0, :HALF], in1=prod[:, :, 1, HALF:], op=ALU.add
             )
-            nc.gpsimd.tensor_tensor(
+            adder.tensor_tensor(
                 out=result[:, :, t, HALF:], in0=prod[:, :, 0, HALF:], in1=prod[:, :, 1, :HALF], op=ALU.add
             )
+            if kind == 0:
+                heads = out_0[b, n * CHUNK_HEADS : (n + 1) * CHUNK_HEADS]
+            else:
+                heads = out_1[b]
+            rows = heads.rearrange("h (p t) d -> p h t d", t=SEQ_TILES)
+            if t == GPSIMD_TILES - 1:
+                nc.sync.dma_start(out=rows[:, :, :GPSIMD_TILES, :], in_=result[:, :, :GPSIMD_TILES, :])
             if t == SEQ_TILES - 1:
-                if kind == 0:
-                    heads = out_0[b, n * CHUNK_HEADS : (n + 1) * CHUNK_HEADS]
-                else:
-                    heads = out_1[b]
-                nc.sync.dma_start(
-                    out=heads.rearrange("h (p t) d -> p h t d", t=SEQ_TILES), in_=result[:]
-                )
+                nc.sync.dma_start(out=rows[:, :, GPSIMD_TILES:, :], in_=result[:, :, GPSIMD_TILES:, :])
 
-        for j in range(CHUNK_HEADS):
-            prepare_w(0, j)
-        for n in range(CHUNKS):
-            for m in range(TOKEN_TILES):
-                if n == 0:
-                    prepare_x(m)
-                if n + 1 < CHUNKS and m >= TOKEN_TILES - CHUNK_HEADS:
-                    prepare_w(n + 1, m - (TOKEN_TILES - CHUNK_HEADS))
-                project(m, n)
+        lead_in(prepare_x, prepare_w)
+        build_tables()
+        all_banks(prepare_x, prepare_w, project)

@@ -213,9 +213,9 @@ def tile_biboattention_pa_kernel(
             for h in range(CHUNK_HEADS):
                 nc.vector.scalar_tensor_tensor(
                     out=prod[:, h, :, :],
-                    in0=acc[:, h * HEAD_DIM : (h + 1) * HEAD_DIM].unsqueeze(1).to_broadcast([P, 2, HEAD_DIM]),
+                    in0=table[:, t, kind, :, :],
                     scalar=factor[:, h : h + 1],
-                    in1=table[:, t, kind, :, :],
+                    in1=acc[:, h * HEAD_DIM : (h + 1) * HEAD_DIM].unsqueeze(1).to_broadcast([P, 2, HEAD_DIM]),
                     op0=ALU.mult,
                     op1=ALU.mult,
                 )

@@ -48,7 +48,8 @@ def tile_biboattention_pa_kernel(
         small = ctx.enter_context(tc.tile_pool(name="small", bufs=4))
         prod_pool = ctx.enter_context(tc.tile_pool(name="prod", bufs=3))
         result_pool = ctx.enter_context(tc.tile_pool(name="result", bufs=3))
-        flip_psum = ctx.enter_context(tc.psum_pool(name="flip_psum", bufs=4))
+        spread_psum = ctx.enter_context(tc.psum_pool(name="spread_psum", bufs=1))
+        flip_psum = ctx.enter_context(tc.psum_pool(name="flip_psum", bufs=3))
         acc_psum = ctx.enter_context(tc.psum_pool(name="acc_psum", bufs=4))
         ctx.enter_context(tc.manual_schedule())
 
@@ -56,6 +57,20 @@ def tile_biboattention_pa_kernel(
         wq_view = wq.rearrange("(n j p) k -> n j p k", j=CHUNK_HEADS, p=P)
         wk_view = wk.rearrange("(j p) k -> j p k", p=P)
 
+        cos_sb = const.tile([P, SEQ_TILES, HEAD_DIM], BF16)
+        sin_sb = const.tile([P, SEQ_TILES, HEAD_DIM], BF16)
+        nc.sync.dma_start(out=cos_sb[:], in_=cos.rearrange("(p t) d -> p t d", t=SEQ_TILES))
+        nc.sync.dma_start(out=sin_sb[:], in_=sin.rearrange("(p t) d -> p t d", t=SEQ_TILES))
+        vectors = const.tile([P, CHUNK], BF16)
+        nc.vector.memset(vectors[:], 0.0)
+        ones = const.tile([P, P], BF16)
+        nc.vector.memset(ones[:], 1.0)
+        nc.sync.dma_start(out=vectors[0:1, 0:HEAD_DIM], in_=q_norm_w.unsqueeze(0))
+        nc.sync.dma_start(out=vectors[0:1, HEAD_DIM : 2 * HEAD_DIM], in_=k_norm_w.unsqueeze(0))
+        nc.sync.dma_start(
+            out=vectors[0:1, 2 * HEAD_DIM : 2 * HEAD_DIM + Q_HEADS],
+            in_=ssmax_scale.rearrange("a h b c -> (a b c) h"),
+        )
         def lead_in(on_x, on_w):
             for j in range(CHUNK_HEADS):
                 on_w(0, j)
@@ -85,20 +100,6 @@ def tile_biboattention_pa_kernel(
         lead_in(load_x, load_w)
         all_banks(load_x, load_w, lambda m, n: None)
 
-        cos_sb = const.tile([P, SEQ_TILES, HEAD_DIM], BF16)
-        sin_sb = const.tile([P, SEQ_TILES, HEAD_DIM], BF16)
-        nc.scalar.dma_start(out=cos_sb[:], in_=cos.rearrange("(p t) d -> p t d", t=SEQ_TILES))
-        nc.scalar.dma_start(out=sin_sb[:], in_=sin.rearrange("(p t) d -> p t d", t=SEQ_TILES))
-        vectors = const.tile([P, CHUNK], BF16)
-        nc.vector.memset(vectors[:], 0.0)
-        ones = const.tile([P, P], BF16)
-        nc.vector.memset(ones[:], 1.0)
-        nc.scalar.dma_start(out=vectors[0:1, 0:HEAD_DIM], in_=q_norm_w.unsqueeze(0))
-        nc.scalar.dma_start(out=vectors[0:1, HEAD_DIM : 2 * HEAD_DIM], in_=k_norm_w.unsqueeze(0))
-        nc.scalar.dma_start(
-            out=vectors[0:1, 2 * HEAD_DIM : 2 * HEAD_DIM + Q_HEADS],
-            in_=ssmax_scale.rearrange("a h b c -> (a b c) h"),
-        )
         ident = const.tile([P, P], F32)
         make_identity(nc, ident[:])
 
@@ -107,15 +108,13 @@ def tile_biboattention_pa_kernel(
         warm = const.tile([P, 1], F32)
         nc.scalar.activation(out=warm[:], in_=one[:], func=ACT.Abs_reciprocal_sqrt)
 
-        gain = const.tile([P, HEADS], F32)
+        spread = spread_psum.tile([P, CHUNK], F32)
+        ssmax = spread[:, 2 * HEAD_DIM : 2 * HEAD_DIM + Q_HEADS]
         table = const.tile([P, SEQ_TILES, 2, 2, HEAD_DIM], F32)
 
         def build_tables():
-          spread = flip_psum.tile([P, CHUNK], F32, name="flipped")
           nc.tensor.matmul(out=spread[:], lhsT=ones[:], rhs=vectors[:], start=True, stop=True)
           norm_w = spread[:, : 2 * HEAD_DIM].rearrange("p (kind d) -> p kind d", kind=2)
-          nc.vector.memset(gain[:, Q_HEADS:], 1.0)
-          nc.vector.tensor_scalar_mul(out=gain[:, :Q_HEADS], in0=spread[:, 2 * HEAD_DIM : 2 * HEAD_DIM + Q_HEADS], scalar1=math.log(SEQ))
           for kind in range(2):
               nc.vector.tensor_tensor(
                   out=table[:, :, kind, 0, :],
@@ -205,10 +204,18 @@ def tile_biboattention_pa_kernel(
             nc.scalar.activation(
                 out=rstd[:], in_=sumsq[:], func=ACT.Abs_reciprocal_sqrt, scale=1.0 / HEAD_DIM, bias=EPS
             )
-            factor = small.tile([P, CHUNK_HEADS], F32)
-            nc.vector.tensor_mul(
-                out=factor[:], in0=rstd[:], in1=gain[:, n * CHUNK_HEADS : (n + 1) * CHUNK_HEADS]
-            )
+            if kind == 0:
+                factor = small.tile([P, CHUNK_HEADS], F32)
+                nc.vector.scalar_tensor_tensor(
+                    out=factor[:],
+                    in0=rstd[:],
+                    scalar=math.log(SEQ),
+                    in1=ssmax[:, n * CHUNK_HEADS : (n + 1) * CHUNK_HEADS],
+                    op0=ALU.mult,
+                    op1=ALU.mult,
+                )
+            else:
+                factor = rstd
             prod = prod_pool.tile([P, CHUNK_HEADS, 2, HEAD_DIM], F32)
             for h in range(CHUNK_HEADS):
                 nc.vector.scalar_tensor_tensor(
@@ -240,6 +247,6 @@ def tile_biboattention_pa_kernel(
             if t == SEQ_TILES - 1:
                 nc.sync.dma_start(out=rows[:, :, GPSIMD_TILES:, :], in_=result[:, :, GPSIMD_TILES:, :])
 
-        lead_in(prepare_x, prepare_w)
         build_tables()
+        lead_in(prepare_x, prepare_w)
         all_banks(prepare_x, prepare_w, project)

from contextlib import ExitStack
import math

import concourse.mybir as mybir
from concourse.masks import make_identity

F32 = mybir.dt.float32
BF16 = mybir.dt.bfloat16
U32 = mybir.dt.uint32
U8 = mybir.dt.uint8
FP8X4 = mybir.dt.float8_e4m3fn_x4
ACT = mybir.ActivationFunctionType
ALU = mybir.AluOpType

P = 128
BATCH, SEQ, HIDDEN = 2, 512, 2048
Q_HEADS, KV_HEADS, HEAD_DIM = 16, 4, 128
HALF = HEAD_DIM // 2
EPS = 1e-6

K_PASS = 4 * P
PASSES = HIDDEN // K_PASS
WORDS_PER_PASS = K_PASS // 2
SEQ_TILES = SEQ // P
TOKEN_TILES = BATCH * SEQ_TILES
CHUNK_HEADS = 4
CHUNK = CHUNK_HEADS * HEAD_DIM
Q_CHUNKS = Q_HEADS // CHUNK_HEADS
CHUNKS = Q_CHUNKS + KV_HEADS // CHUNK_HEADS
HEADS = Q_HEADS + KV_HEADS
ROW_TILES = TOKEN_TILES + CHUNKS * CHUNK_HEADS

X_LEAD = 2
GPSIMD_TILES = 3

FLOPS = 2 * BATCH * SEQ * HIDDEN * HEADS * HEAD_DIM


def tile_biboattention_pa_kernel(
    tc, hidden_states, cos, sin, wq, wk, q_norm_w, k_norm_w, ssmax_scale, out_0, out_1
):
    nc = tc.nc
    with ExitStack() as ctx:
        const = ctx.enter_context(tc.tile_pool(name="const", bufs=1))
        raw_pool = ctx.enter_context(tc.tile_pool(name="raw", bufs=ROW_TILES))
        grouped_pool = ctx.enter_context(tc.tile_pool(name="grouped", bufs=3))
        w_pool = ctx.enter_context(tc.tile_pool(name="w_mx", bufs=3))
        small = ctx.enter_context(tc.tile_pool(name="small", bufs=4))
        prod_pool = ctx.enter_context(tc.tile_pool(name="prod", bufs=3))
        result_pool = ctx.enter_context(tc.tile_pool(name="result", bufs=3))
        spread_psum = ctx.enter_context(tc.psum_pool(name="spread_psum", bufs=1))
        flip_psum = ctx.enter_context(tc.psum_pool(name="flip_psum", bufs=3))
        acc_psum = ctx.enter_context(tc.psum_pool(name="acc_psum", bufs=4))
        ctx.enter_context(tc.manual_schedule())

        x_view = hidden_states.rearrange("b (p t) k -> b t p k", t=SEQ_TILES)
        wq_view = wq.rearrange("(n j p) k -> n j p k", j=CHUNK_HEADS, p=P)
        wk_view = wk.rearrange("(j p) k -> j p k", p=P)

        cos_sb = const.tile([P, SEQ_TILES, HEAD_DIM], BF16)
        sin_sb = const.tile([P, SEQ_TILES, HEAD_DIM], BF16)
        nc.sync.dma_start(out=cos_sb[:], in_=cos.rearrange("(p t) d -> p t d", t=SEQ_TILES))
        nc.sync.dma_start(out=sin_sb[:], in_=sin.rearrange("(p t) d -> p t d", t=SEQ_TILES))
        vectors = const.tile([P, CHUNK], BF16)
        nc.vector.memset(vectors[:], 0.0)
        ones = const.tile([P, P], BF16)
        nc.vector.memset(ones[:], 1.0)
        nc.sync.dma_start(out=vectors[0:1, 0:HEAD_DIM], in_=q_norm_w.unsqueeze(0))
        nc.sync.dma_start(out=vectors[0:1, HEAD_DIM : 2 * HEAD_DIM], in_=k_norm_w.unsqueeze(0))
        nc.sync.dma_start(
            out=vectors[0:1, 2 * HEAD_DIM : 2 * HEAD_DIM + Q_HEADS],
            in_=ssmax_scale.rearrange("a h b c -> (a b c) h"),
        )
        def lead_in(on_x, on_w):
            for j in range(CHUNK_HEADS):
                on_w(0, j)
            for m in range(X_LEAD):
                on_x(m)

        def all_banks(on_x, on_w, on_bank):
            for n in range(CHUNKS):
                for m in range(TOKEN_TILES):
                    if n == 0 and m + X_LEAD < TOKEN_TILES:
                        on_x(m + X_LEAD)
                    if n + 1 < CHUNKS and m < CHUNK_HEADS:
                        on_w(n + 1, m)
                    on_bank(m, n)

        x_raw = {}
        w_raw = {}

        def load_x(m):
            x_raw[m] = raw_pool.tile([P, HIDDEN], BF16, name="raw")
            nc.sync.dma_start(out=x_raw[m][:], in_=x_view[m // SEQ_TILES, m % SEQ_TILES])

        def load_w(n, j):
            w_raw[n, j] = raw_pool.tile([P, HIDDEN], BF16, name="raw")
            nc.sync.dma_start(out=w_raw[n, j][:], in_=wq_view[n, j] if n < Q_CHUNKS else wk_view[j])

        lead_in(load_x, load_w)
        all_banks(load_x, load_w, lambda m, n: None)

        ident = const.tile([P, P], F32)
        make_identity(nc, ident[:])

        one = const.tile([P, 1], F32)
        nc.vector.memset(one[:], 1.0)
        warm = const.tile([P, 1], F32)
        nc.scalar.activation(out=warm[:], in_=one[:], func=ACT.Abs_reciprocal_sqrt)

        spread = spread_psum.tile([P, CHUNK], F32)
        ssmax = spread[:, 2 * HEAD_DIM : 2 * HEAD_DIM + Q_HEADS]
        table = const.tile([P, SEQ_TILES, 2, 2, HEAD_DIM], F32)

        def build_tables():
          nc.tensor.matmul(out=spread[:], lhsT=ones[:], rhs=vectors[:], start=True, stop=True)
          norm_w = spread[:, : 2 * HEAD_DIM].rearrange("p (kind d) -> p kind d", kind=2)
          for kind in range(2):
              nc.vector.tensor_tensor(
                  out=table[:, :, kind, 0, :],
                  in0=cos_sb[:],
                  in1=norm_w[:, kind, :].unsqueeze(1).to_broadcast([P, SEQ_TILES, HEAD_DIM]),
                  op=ALU.mult,
              )
              nc.vector.tensor_tensor(
                  out=table[:, :, kind, 1, :HALF],
                  in0=sin_sb[:, :, HALF:],
                  in1=norm_w[:, kind, :HALF].unsqueeze(1).to_broadcast([P, SEQ_TILES, HALF]),
                  op=ALU.mult,
              )
              nc.vector.scalar_tensor_tensor(
                  out=table[:, :, kind, 1, HALF:],
                  in0=sin_sb[:, :, :HALF],
                  scalar=-1.0,
                  in1=norm_w[:, kind, HALF:].unsqueeze(1).to_broadcast([P, SEQ_TILES, HALF]),
                  op0=ALU.mult,
                  op1=ALU.mult,
              )

        x_codes = const.tile([P, TOKEN_TILES, PASSES, P], U32, align_bytes=64)
        x_scales = const.tile([P, TOKEN_TILES, PASSES, P], U8, align_bytes=64)

        def quantise_row_tile(raw, codes, scales):
            words = raw[:].bitcast(F32)
            grouped = grouped_pool.tile([P, PASSES, P, 2], F32, align_bytes=64)
            for bank in range(PASSES // 2):
                flipped = flip_psum.tile([P, 2, 2, P], F32)
                for a in range(2):
                    for u in range(2):
                        first = (2 * bank + a) * WORDS_PER_PASS + u * P
                        nc.tensor.transpose(flipped[:, a, u, :], words[:, first : first + P], ident[:])
                nc.scalar.copy(
                    out=grouped[:, 2 * bank : 2 * bank + 2, :, :],
                    in_=flipped[:].rearrange("p a u r -> p a r u"),
                )
            for g in range(PASSES):
                nc.vector.quantize_mx(
                    out=codes[:, g, :].bitcast(FP8X4),
                    scales=scales[:, g, :],
                    in_=grouped[:, g, :, :].rearrange("p r u -> p (r u)").bitcast(BF16),
                )

        w_mx = {}

        def prepare_w(n, j):
            if j == 0:
                w_codes = w_pool.tile([P, PASSES, CHUNK], U32, align_bytes=64)
                w_scales = w_pool.tile([P, PASSES, CHUNK], U8, align_bytes=64)
                w_mx[n] = (w_codes, w_scales)
            w_codes, w_scales = w_mx[n]
            rows = slice(j * P, (j + 1) * P)
            quantise_row_tile(w_raw[n, j], w_codes[:, :, rows], w_scales[:, :, rows])

        def prepare_x(m):
            quantise_row_tile(x_raw[m], x_codes[:, m], x_scales[:, m])

        results = {}

        def project(m, n):
            b, t = m // SEQ_TILES, m % SEQ_TILES
            kind = 0 if n < Q_CHUNKS else 1
            w_codes, w_scales = w_mx[n]
            acc = acc_psum.tile([P, CHUNK], F32)
            for g in range(PASSES):
                nc.tensor.matmul_mx(
                    out=acc[:],
                    lhsT=x_codes[:, m, g, :].bitcast(FP8X4),
                    lhsT_scale=x_scales[:, m, g, :],
                    rhs=w_codes[:, g, :].bitcast(FP8X4),
                    rhs_scale=w_scales[:, g, :],
                    start=(g == 0),
                    stop=(g == PASSES - 1),
                )
            sumsq = small.tile([P, CHUNK_HEADS], F32)
            for h in range(CHUNK_HEADS):
                squares = small.tile([P, HEAD_DIM], F32)
                nc.scalar.activation(
                    out=squares[:],
                    in_=acc[:, h * HEAD_DIM : (h + 1) * HEAD_DIM],
                    func=ACT.Square,
                    accum_out=sumsq[:, h : h + 1],
                )
            rstd = small.tile([P, CHUNK_HEADS], F32)
            nc.scalar.activation(
                out=rstd[:], in_=sumsq[:], func=ACT.Abs_reciprocal_sqrt, scale=1.0 / HEAD_DIM, bias=EPS
            )
            if kind == 0:
                factor = small.tile([P, CHUNK_HEADS], F32)
                nc.vector.scalar_tensor_tensor(
                    out=factor[:],
                    in0=rstd[:],
                    scalar=math.log(SEQ),
                    in1=ssmax[:, n * CHUNK_HEADS : (n + 1) * CHUNK_HEADS],
                    op0=ALU.mult,
                    op1=ALU.mult,
                )
            else:
                factor = rstd
            prod = prod_pool.tile([P, CHUNK_HEADS, 2, HEAD_DIM], F32)
            for h in range(CHUNK_HEADS):
                nc.vector.scalar_tensor_tensor(
                    out=prod[:, h, :, :],
                    in0=table[:, t, kind, :, :],
                    scalar=factor[:, h : h + 1],
                    in1=acc[:, h * HEAD_DIM : (h + 1) * HEAD_DIM].unsqueeze(1).to_broadcast([P, 2, HEAD_DIM]),
                    op0=ALU.mult,
                    op1=ALU.mult,
                )
            if t == 0:
                result = result_pool.tile([P, CHUNK_HEADS, SEQ_TILES, HEAD_DIM], F32)
                results[0] = result
            result = results[0]
            adder = nc.gpsimd if t < GPSIMD_TILES else nc.vector
            adder.tensor_tensor(
                out=result[:, :, t, :HALF], in0=prod[:, :, 0, :HALF], in1=prod[:, :, 1, HALF:], op=ALU.add
            )
            adder.tensor_tensor(
                out=result[:, :, t, HALF:], in0=prod[:, :, 0, HALF:], in1=prod[:, :, 1, :HALF], op=ALU.add
            )
            if kind == 0:
                heads = out_0[b, n * CHUNK_HEADS : (n + 1) * CHUNK_HEADS]
            else:
                heads = out_1[b]
            rows = heads.rearrange("h (p t) d -> p h t d", t=SEQ_TILES)
            if t == GPSIMD_TILES - 1:
                nc.sync.dma_start(out=rows[:, :, :GPSIMD_TILES, :], in_=result[:, :, :GPSIMD_TILES, :])
            if t == SEQ_TILES - 1:
                nc.sync.dma_start(out=rows[:, :, GPSIMD_TILES:, :], in_=result[:, :, GPSIMD_TILES:, :])

        build_tables()
        lead_in(prepare_x, prepare_w)
        all_banks(prepare_x, prepare_w, project)
